import numpy as np
import ml_dtypes

BF16 = ml_dtypes.bfloat16


def bf(x):
    return np.asarray(x, np.float32).astype(BF16)


def f32(x):
    return np.asarray(x, np.float32)


def f64(x):
    return np.asarray(x).astype(np.float64)


def striped(idx):
    return np.tile(idx.reshape(-1, 16).T, (8, 1))


T, S, N = 128, 512, 512


def ring(n):
    p = np.random.permutation(n)
    idx = np.empty(n, p.dtype)
    idx[p] = np.roll(p, -1)
    return idx


def setup_inputs():
    return {"x": bf(np.random.standard_normal((T, S))), "weight": bf(np.random.standard_normal((T, T)) / np.sqrt(T)), "bias": f32(0.1 * np.random.standard_normal((T, 1))), "offs": striped(ring(S)[:N])}


def reference(x, weight, bias, offs):
    idx = offs[:16].T.reshape(-1)
    return f64(weight).T @ f64(x)[:, idx] + f64(bias)

@@ -1,0 +1,33 @@
+import concourse.mybir as mybir
+
+P = 128
+S = 512
+N = 512
+FLOPS = 2 * P * P * N
+
+BF16, F32, U16 = mybir.dt.bfloat16, mybir.dt.float32, mybir.dt.uint16
+
+
+def tile_graphembedding_kernel(tc, x, weight, bias, offs, out):
+    nc = tc.nc
+    with (
+        tc.tile_pool(name="held", bufs=1) as held,
+        tc.psum_pool(name="psum", bufs=1) as psum,
+    ):
+        offsets = held.tile([P, N // 16], U16, name="offsets")
+        nc.sync.dma_start(offsets[:], offs)
+        series = held.tile([P, S], BF16, name="series")
+        nc.sync.dma_start(series[:], x)
+        projection = held.tile([P, P], BF16, name="projection")
+        nc.sync.dma_start(projection[:], weight)
+        bias_column = held.tile([P, 1], F32, name="bias_column")
+        nc.sync.dma_start(bias_column[:], bias)
+
+        product = psum.tile([P, N], F32, name="product")
+        nc.tensor.matmul(
+            product[:], projection[:], series[:].indirect(offsets[:]), start=True, stop=True
+        )
+
+        result = held.tile([P, N], F32, name="result")
+        nc.vector.tensor_scalar_add(result[:], product[:], bias_column[:])
+        nc.sync.dma_start(out, result[:])

@@ -17,11 +17,11 @@ def tile_graphembedding_kernel(tc, x, weight, bias, offs, out):
         offsets = held.tile([P, N // 16], U16, name="offsets")
         nc.sync.dma_start(offsets[:], offs)
         series = held.tile([P, S], BF16, name="series")
-        nc.sync.dma_start(series[:], x)
+        nc.scalar.dma_start(series[:], x)
         projection = held.tile([P, P], BF16, name="projection")
         nc.sync.dma_start(projection[:], weight)
         bias_column = held.tile([P, 1], F32, name="bias_column")
-        nc.sync.dma_start(bias_column[:], bias)
+        nc.scalar.dma_start(bias_column[:], bias)
 
         product = psum.tile([P, N], F32, name="product")
         nc.tensor.matmul(

@@ -3,9 +3,12 @@ import concourse.mybir as mybir
 P = 128
 S = 512
 N = 512
+PIECES = 4
+W = N // PIECES
 FLOPS = 2 * P * P * N
 
 BF16, F32, U16 = mybir.dt.bfloat16, mybir.dt.float32, mybir.dt.uint16
+IDENTITY = mybir.ActivationFunctionType.Identity
 
 
 def tile_graphembedding_kernel(tc, x, weight, bias, offs, out):
@@ -23,11 +26,18 @@ def tile_graphembedding_kernel(tc, x, weight, bias, offs, out):
         bias_column = held.tile([P, 1], F32, name="bias_column")
         nc.scalar.dma_start(bias_column[:], bias)
 
-        product = psum.tile([P, N], F32, name="product")
-        nc.tensor.matmul(
-            product[:], projection[:], series[:].indirect(offsets[:]), start=True, stop=True
-        )
+        for piece in range(PIECES):
+            product = psum.tile([P, W], F32, name=f"product{piece}")
+            piece_offsets = offsets[:, piece * (W // 16) : (piece + 1) * (W // 16)]
+            nc.tensor.matmul(
+                product[:], projection[:], series[:].indirect(piece_offsets), start=True, stop=True
+            )
 
-        result = held.tile([P, N], F32, name="result")
-        nc.vector.tensor_scalar_add(result[:], product[:], bias_column[:])
-        nc.sync.dma_start(out, result[:])
+            result = held.tile([P, W], F32, name=f"result{piece}")
+            columns = out[:, piece * W : (piece + 1) * W]
+            if piece % 2 == 0:
+                nc.vector.tensor_scalar_add(result[:], product[:], bias_column[:])
+                nc.sync.dma_start(columns, result[:])
+            else:
+                nc.scalar.activation(result[:], product[:], IDENTITY, bias=bias_column[:])
+                nc.scalar.dma_start(columns, result[:])

@@ -3,7 +3,7 @@ import concourse.mybir as mybir
 P = 128
 S = 512
 N = 512
-PIECES = 4
+PIECES = 2
 W = N // PIECES
 FLOPS = 2 * P * P * N
 

@@ -3,12 +3,11 @@ import concourse.mybir as mybir
 P = 128
 S = 512
 N = 512
-PIECES = 2
+PIECES = 4
 W = N // PIECES
 FLOPS = 2 * P * P * N
 
 BF16, F32, U16 = mybir.dt.bfloat16, mybir.dt.float32, mybir.dt.uint16
-IDENTITY = mybir.ActivationFunctionType.Identity
 
 
 def tile_graphembedding_kernel(tc, x, weight, bias, offs, out):
@@ -34,10 +33,7 @@ def tile_graphembedding_kernel(tc, x, weight, bias, offs, out):
             )
 
             result = held.tile([P, W], F32, name=f"result{piece}")
-            columns = out[:, piece * W : (piece + 1) * W]
-            if piece % 2 == 0:
-                nc.vector.tensor_scalar_add(result[:], product[:], bias_column[:])
-                nc.sync.dma_start(columns, result[:])
-            else:
-                nc.scalar.activation(result[:], product[:], IDENTITY, bias=bias_column[:])
-                nc.scalar.dma_start(columns, result[:])
+            nc.vector.tensor_scalar_add(result[:], product[:], bias_column[:])
+
+            store_queue = nc.sync if piece % 2 == 0 else nc.scalar
+            store_queue.dma_start(out[:, piece * W : (piece + 1) * W], result[:])

@@ -16,12 +16,12 @@ def tile_graphembedding_kernel(tc, x, weight, bias, offs, out):
         tc.tile_pool(name="held", bufs=1) as held,
         tc.psum_pool(name="psum", bufs=1) as psum,
     ):
+        series = held.tile([P, S], BF16, name="series")
+        nc.sync.dma_start(series[:], x)
         offsets = held.tile([P, N // 16], U16, name="offsets")
         nc.sync.dma_start(offsets[:], offs)
-        series = held.tile([P, S], BF16, name="series")
-        nc.scalar.dma_start(series[:], x)
         projection = held.tile([P, P], BF16, name="projection")
-        nc.sync.dma_start(projection[:], weight)
+        nc.scalar.dma_start(projection[:], weight)
         bias_column = held.tile([P, 1], F32, name="bias_column")
         nc.scalar.dma_start(bias_column[:], bias)
 

@@ -3,8 +3,7 @@ import concourse.mybir as mybir
 P = 128
 S = 512
 N = 512
-PIECES = 4
-W = N // PIECES
+WIDTHS = (96, 96, 192, 128)
 FLOPS = 2 * P * P * N
 
 BF16, F32, U16 = mybir.dt.bfloat16, mybir.dt.float32, mybir.dt.uint16
@@ -25,15 +24,17 @@ def tile_graphembedding_kernel(tc, x, weight, bias, offs, out):
         bias_column = held.tile([P, 1], F32, name="bias_column")
         nc.scalar.dma_start(bias_column[:], bias)
 
-        for piece in range(PIECES):
-            product = psum.tile([P, W], F32, name=f"product{piece}")
-            piece_offsets = offsets[:, piece * (W // 16) : (piece + 1) * (W // 16)]
+        first = 0
+        for piece, width in enumerate(WIDTHS):
+            product = psum.tile([P, width], F32, name=f"product{piece}")
+            piece_offsets = offsets[:, first // 16 : (first + width) // 16]
             nc.tensor.matmul(
                 product[:], projection[:], series[:].indirect(piece_offsets), start=True, stop=True
             )
 
-            result = held.tile([P, W], F32, name=f"result{piece}")
+            result = held.tile([P, width], F32, name=f"result{piece}")
             nc.vector.tensor_scalar_add(result[:], product[:], bias_column[:])
 
             store_queue = nc.sync if piece % 2 == 0 else nc.scalar
-            store_queue.dma_start(out[:, piece * W : (piece + 1) * W], result[:])
+            store_queue.dma_start(out[:, first : first + width], result[:])
+            first += width

import concourse.mybir as mybir

P = 128
S = 512
N = 512
WIDTHS = (96, 96, 192, 128)
FLOPS = 2 * P * P * N

BF16, F32, U16 = mybir.dt.bfloat16, mybir.dt.float32, mybir.dt.uint16


def tile_graphembedding_kernel(tc, x, weight, bias, offs, out):
    nc = tc.nc
    with (
        tc.tile_pool(name="held", bufs=1) as held,
        tc.psum_pool(name="psum", bufs=1) as psum,
    ):
        series = held.tile([P, S], BF16, name="series")
        nc.sync.dma_start(series[:], x)
        offsets = held.tile([P, N // 16], U16, name="offsets")
        nc.sync.dma_start(offsets[:], offs)
        projection = held.tile([P, P], BF16, name="projection")
        nc.scalar.dma_start(projection[:], weight)
        bias_column = held.tile([P, 1], F32, name="bias_column")
        nc.scalar.dma_start(bias_column[:], bias)

        first = 0
        for piece, width in enumerate(WIDTHS):
            product = psum.tile([P, width], F32, name=f"product{piece}")
            piece_offsets = offsets[:, first // 16 : (first + width) // 16]
            nc.tensor.matmul(
                product[:], projection[:], series[:].indirect(piece_offsets), start=True, stop=True
            )

            result = held.tile([P, width], F32, name=f"result{piece}")
            nc.vector.tensor_scalar_add(result[:], product[:], bias_column[:])

            store_queue = nc.sync if piece % 2 == 0 else nc.scalar
            store_queue.dma_start(out[:, first : first + width], result[:])
            first += width
